import numpy as np
import ml_dtypes


def mxq(x, axis, fmt="e4m3"):
    dtype, down = {"e4m3": (ml_dtypes.float8_e4m3fn, 7), "e5m2": (ml_dtypes.float8_e5m2, 14)}[fmt]
    v = np.moveaxis(np.asarray(x, np.float32).astype(ml_dtypes.bfloat16).astype(np.float64), axis, -1)
    blocks = v.reshape(v.shape[:-1] + (-1, 32))
    amax = np.abs(blocks).max(-1, keepdims=True)
    byte = np.maximum(np.where(amax > 0, np.frexp(amax)[1] - 1 + 127, 0) - down, 1)
    scale = np.exp2(byte - 127.0)
    codes = (blocks / scale).astype(np.float32).astype(dtype).astype(np.float64)
    return np.moveaxis((codes * scale).reshape(v.shape), -1, axis)


WIDE = False


def mx_kscale(k):
    if not WIDE:
        return np.ones(k)
    levels = np.array([10, -10, 5, -5, 0])
    a = np.random.permutation(np.resize(levels, k // 512 * 4)).reshape(k // 512, 4)
    idx = np.arange(k)
    return np.exp2(a[idx // 512, idx % 128 // 32])


BF16 = ml_dtypes.bfloat16


def bf(x):
    return np.asarray(x, np.float32).astype(BF16)


def f64(x):
    return np.asarray(x).astype(np.float64)


R, C, B, E, H = 4, 512, 1, 1024, 8
D = E // H


def setup_inputs():
    s, t = mx_kscale(E), mx_kscale(E)
    return {"x": bf(np.random.standard_normal((R, C, B, E)) * s),
            "Wq": bf(np.random.standard_normal((E, E)) * 1.4 / np.sqrt(E) / s[:, None] * t),
            "bq": bf(np.random.standard_normal(E) * 0.3 * t),
            "k": bf(np.random.standard_normal((R, C, B, H, D)) * 1.4 / t.reshape(H, D))}


def reference(x, Wq, bq, k):
    scaling = D ** -0.5 / np.sqrt(R)
    q = ((mxq(f64(x), 3, "e4m3") @ mxq(f64(Wq), 0, "e4m3")) + f64(bq)) * scaling
    qh = q.reshape(R, C, B, H, D).transpose(3, 2, 1, 0, 4).reshape(H, B, C, R * D)
    kh = f64(k).transpose(3, 2, 0, 4, 1).reshape(H, B, R * D, C)
    sc = mxq(qh, 3, "e4m3") @ mxq(kh, 2, "e4m3")
    e = np.exp(sc - sc.max(-1, keepdims=True))
    return e / e.sum(-1, keepdims=True)

@@ -1,0 +1,279 @@
+import math
+from contextlib import ExitStack
+
+import concourse.mybir as mybir
+from concourse.masks import make_identity
+
+F32 = mybir.dt.float32
+BF16 = mybir.dt.bfloat16
+U32 = mybir.dt.uint32
+U8 = mybir.dt.uint8
+FP8X4 = mybir.dt.float8_e4m3fn_x4
+ACT = mybir.ActivationFunctionType
+ALU = mybir.AluOpType
+AXIS = mybir.AxisListType
+
+P = 128
+PACK = 4
+K_PASS = P * PACK
+
+ROWS = 4
+COLS = 512
+WIDTH = 1024
+HEADS = 8
+HEAD_DIM = WIDTH // HEADS
+PASSES = WIDTH // K_PASS
+COL_BLOCKS = COLS // P
+SUB = P // ROWS
+SUBS = P // SUB
+HEAD_GROUP = 4
+HEAD_GROUPS = HEADS // HEAD_GROUP
+GROUP_COLS = HEAD_GROUP * HEAD_DIM
+
+FLOPS = 2 * ROWS * COLS * WIDTH * WIDTH + 2 * HEADS * COLS * COLS * ROWS * HEAD_DIM
+
+
+def tile_rowselfattention_pa_kernel(tc, x, Wq, bq, k, out):
+    nc = tc.nc
+    factor = 1.0 / math.sqrt(HEAD_DIM * ROWS)
+
+    x_rows = x.rearrange("r i b e -> r (i b) e")
+    k_rows = k.rearrange("r j b h d -> r (j b) (h d)")
+    out_rows = out.rearrange("h b i j -> h (b i) j")
+
+    with ExitStack() as stack:
+        const = stack.enter_context(tc.tile_pool(name="const", bufs=1))
+        raw = stack.enter_context(tc.tile_pool(name="raw", bufs=2 * COL_BLOCKS + PASSES))
+        keep = stack.enter_context(tc.tile_pool(name="keep", bufs=1))
+        grouped_pool = stack.enter_context(tc.tile_pool(name="grouped", bufs=4))
+        soft = stack.enter_context(tc.tile_pool(name="soft", bufs=8))
+        psum_t = stack.enter_context(tc.psum_pool(name="psum_t", bufs=2))
+        psum_q = stack.enter_context(tc.psum_pool(name="psum_q", bufs=3))
+        psum_s = stack.enter_context(tc.psum_pool(name="psum_s", bufs=3))
+
+        ident_f32 = const.tile([P, P], F32)
+        make_identity(nc, ident_f32[:])
+        ident_bf16 = const.tile([P, P], BF16)
+        make_identity(nc, ident_bf16[:])
+        warm = const.tile([P, 1], F32)
+        nc.vector.memset(warm[:], 0.0)
+        nc.scalar.activation(out=warm[:], in_=warm[:], func=ACT.Exp)
+        bias_rows = const.tile([P, P], BF16)
+        nc.vector.memset(bias_rows[:], 0.0)
+
+        def load_columns(rows, block):
+            raw_tile = raw.tile([P, SUBS, WIDTH], BF16, tag="raw")
+            for r in range(ROWS):
+                nc.sync.dma_start(
+                    out=raw_tile[r:P:ROWS, :, :],
+                    in_=rows[r, block * P : (block + 1) * P, :].rearrange("(s c) e -> c s e", c=SUB),
+                )
+            return raw_tile
+
+        def load_weight_rows(g):
+            raw_tile = raw.tile([P, 2, 2 * WIDTH], BF16, tag="raw")
+            nc.sync.dma_start(
+                out=raw_tile[:],
+                in_=Wq[g * K_PASS : (g + 1) * K_PASS, :].rearrange("(u p v) c -> p u (v c)", u=2, v=2),
+            )
+            return raw_tile
+
+        x_raw = [load_columns(x_rows, 0)]
+        nc.sync.dma_start(out=bias_rows[0:HEADS, :], in_=bq.rearrange("(h d) -> h d", d=HEAD_DIM))
+        w_raw = [load_weight_rows(g) for g in range(PASSES)]
+        k_raw = [load_columns(k_rows, block) for block in range(COL_BLOCKS)]
+        x_raw.extend([load_columns(x_rows, block) for block in range(1, COL_BLOCKS)])
+
+        x_codes = []
+        x_scales = []
+
+        def prepare_x(block):
+            words_in = x_raw[block][:].bitcast(F32)
+            codes = keep.tile([P, PASSES, COLS], U32, tag="x_codes", bufs=COL_BLOCKS, align_bytes=64)
+            scales = keep.tile([P, PASSES, COLS], U8, tag="x_scales", bufs=COL_BLOCKS, align_bytes=64)
+            for g in range(PASSES):
+                grouped = grouped_pool.tile([P, COLS, PACK], BF16, tag="grouped", align_bytes=64)
+                grouped_words = grouped[:].bitcast(F32)
+                for half in range(2):
+                    bank = psum_t.tile([P, 2, 2, P], F32, tag="t")
+                    for s in range(2):
+                        for u in range(2):
+                            first = (2 * g + u) * P
+                            nc.tensor.transpose(
+                                bank[:, s, u, :],
+                                words_in[:, 2 * half + s, first : first + P],
+                                ident_f32[:],
+                            )
+                    target = grouped_words[:, half * 2 * P : (half + 1) * 2 * P, :]
+                    target = target.rearrange("p (s c) u -> p s c u", s=2)
+                    source = bank[:].rearrange("p s u c -> p s c u")
+                    if half == 0:
+                        nc.vector.tensor_copy(out=target, in_=source)
+                    else:
+                        nc.scalar.copy(out=target, in_=source)
+                nc.vector.quantize_mx(
+                    out=codes[:, g, :].bitcast(FP8X4),
+                    scales=scales[:, g, :],
+                    in_=grouped[:].rearrange("p c t -> p (c t)"),
+                )
+            x_codes.append(codes)
+            x_scales.append(scales)
+
+        w_codes = []
+        w_scales = []
+
+        def prepare_weights(group):
+            codes = keep.tile([P, PASSES, GROUP_COLS], U32, tag="w_codes", bufs=HEAD_GROUPS, align_bytes=64)
+            scales = keep.tile([P, PASSES, GROUP_COLS], U8, tag="w_scales", bufs=HEAD_GROUPS, align_bytes=64)
+            for g in range(PASSES):
+                four_rows = w_raw[g][:].rearrange("p u (v c) -> p (u v) c", v=2)
+                four_rows = four_rows[:, :, group * GROUP_COLS : (group + 1) * GROUP_COLS]
+                grouped = grouped_pool.tile([P, GROUP_COLS, PACK], BF16, tag="grouped", align_bytes=64)
+                if group == 0:
+                    nc.vector.tensor_copy(out=grouped[:], in_=four_rows.rearrange("p t c -> p c t"))
+                else:
+                    nc.scalar.copy(out=grouped[:], in_=four_rows.rearrange("p t c -> p c t"))
+                nc.vector.quantize_mx(
+                    out=codes[:, g, :].bitcast(FP8X4),
+                    scales=scales[:, g, :],
+                    in_=grouped[:].rearrange("p c t -> p (c t)"),
+                )
+            w_codes.append(codes)
+            w_scales.append(scales)
+
+        q_codes = []
+        q_scales = []
+
+        def project(block):
+            block_codes = []
+            block_scales = []
+            for group in range(HEAD_GROUPS):
+                q_grouped = grouped_pool.tile([P, HEAD_GROUP, COLS], BF16, tag="grouped", align_bytes=64)
+                for member in range(HEAD_GROUP):
+                    h = group * HEAD_GROUP + member
+                    head_cols = slice(member * HEAD_DIM, (member + 1) * HEAD_DIM)
+                    acc = psum_q.tile([P, COLS], F32, tag="acc")
+                    for g in range(PASSES):
+                        nc.tensor.matmul_mx(
+                            out=acc[:],
+                            lhsT=w_codes[group][:, g, head_cols].bitcast(FP8X4),
+                            lhsT_scale=w_scales[group][:, g, head_cols],
+                            rhs=x_codes[block][:, g, :].bitcast(FP8X4),
+                            rhs_scale=x_scales[block][:, g, :],
+                            start=(g == 0),
+                            stop=(g == PASSES - 1),
+                        )
+                    if h % 2 == 0:
+                        nc.scalar.activation(
+                            out=q_grouped[:, member, :],
+                            in_=acc[:],
+                            func=ACT.Identity,
+                            bias=bias_scaled[:, h : h + 1],
+                            scale=factor,
+                        )
+                    else:
+                        nc.vector.tensor_scalar(
+                            out=q_grouped[:, member, :],
+                            in0=acc[:],
+                            scalar1=factor,
+                            scalar2=bias_scaled[:, h : h + 1],
+                            op0=ALU.mult,
+                            op1=ALU.add,
+                        )
+                codes = keep.tile([P, HEAD_GROUP * P], U32, tag="q_codes", bufs=COL_BLOCKS * HEAD_GROUPS, align_bytes=64)
+                scales = keep.tile([P, HEAD_GROUP * P], U8, tag="q_scales", bufs=COL_BLOCKS * HEAD_GROUPS, align_bytes=64)
+                nc.vector.quantize_mx(
+                    out=codes[:].bitcast(FP8X4),
+                    scales=scales[:],
+                    in_=q_grouped[:].rearrange("p h c -> p (h c)"),
+                )
+                block_codes.append(codes)
+                block_scales.append(scales)
+            q_codes.append(block_codes)
+            q_scales.append(block_scales)
+
+        k_codes = [
+            keep.tile([P, COLS], U32, tag="k_codes", bufs=HEADS, align_bytes=64, name="k_codes%d" % h)
+            for h in range(HEADS)
+        ]
+        k_scales = [
+            keep.tile([P, COLS], U8, tag="k_scales", bufs=HEADS, align_bytes=64, name="k_scales%d" % h)
+            for h in range(HEADS)
+        ]
+
+        def prepare_k(block):
+            word_cols = slice(block * P, (block + 1) * P)
+            for pair in range(HEADS // 2):
+                bank = psum_t.tile([P, 2, SUBS, P], BF16, tag="t")
+                for member in range(2):
+                    h = 2 * pair + member
+                    for s in range(SUBS):
+                        nc.tensor.transpose(
+                            bank[:, member, s, :],
+                            k_raw[block][:, s, h * HEAD_DIM : (h + 1) * HEAD_DIM],
+                            ident_bf16[:],
+                        )
+                k_grouped = grouped_pool.tile([P, 2, PACK * P], BF16, tag="k_grouped", align_bytes=64)
+                nc.scalar.copy(out=k_grouped[:], in_=bank[:].rearrange("p h s c -> p h (s c)"))
+                for member in range(2):
+                    h = 2 * pair + member
+                    nc.vector.quantize_mx(
+                        out=k_codes[h][:, word_cols].bitcast(FP8X4),
+                        scales=k_scales[h][:, word_cols],
+                        in_=k_grouped[:, member, :],
+                    )
+
+        def attend(block):
+            for h in range(HEADS):
+                group = h // HEAD_GROUP
+                member = h % HEAD_GROUP
+                head_words = slice(member * P, (member + 1) * P)
+                scores = psum_s.tile([P, COLS], F32, tag="scores")
+                nc.tensor.matmul_mx(
+                    out=scores[:],
+                    lhsT=q_codes[block][group][:, head_words].bitcast(FP8X4),
+                    lhsT_scale=q_scales[block][group][:, head_words],
+                    rhs=k_codes[h][:].bitcast(FP8X4),
+                    rhs_scale=k_scales[h][:],
+                    start=True,
+                    stop=True,
+                )
+                neg_max = soft.tile([P, 1], F32, tag="neg_max")
+                nc.vector.tensor_reduce(out=neg_max[:], in_=scores[:], axis=AXIS.X, op=ALU.max, negate=True)
+                weights = soft.tile([P, COLS], F32, tag="weights")
+                total = soft.tile([P, 1], F32, tag="total")
+                nc.scalar.activation(
+                    out=weights[:],
+                    in_=scores[:],
+                    func=ACT.Exp,
+                    bias=neg_max[:, 0:1],
+                    scale=1.0,
+                    accum_out=total[:],
+                )
+                inverse = soft.tile([P, 1], F32, tag="inverse")
+                nc.vector.reciprocal(out=inverse[:], in_=total[:])
+                nc.gpsimd.tensor_scalar(
+                    out=weights[:],
+                    in0=weights[:],
+                    scalar1=inverse[:, 0:1],
+                    scalar2=0.0,
+                    op0=ALU.mult,
+                    op1=ALU.add,
+                )
+                nc.sync.dma_start(out=out_rows[h, block * P : (block + 1) * P, :], in_=weights[:])
+
+        prepare_x(0)
+        for group in range(HEAD_GROUPS):
+            prepare_weights(group)
+        bias_bank = psum_t.tile([P, P], BF16, tag="t")
+        nc.tensor.transpose(bias_bank[:], bias_rows[:], ident_bf16[:])
+        bias_scaled = const.tile([P, HEADS], F32)
+        nc.vector.tensor_scalar_mul(out=bias_scaled[:], in0=bias_bank[:, 0:HEADS], scalar1=factor)
+        project(0)
+        for block in range(COL_BLOCKS):
+            prepare_k(block)
+        for block in range(COL_BLOCKS):
+            if block + 1 < COL_BLOCKS:
+                prepare_x(block + 1)
+                project(block + 1)
+            attend(block)

@@ -30,6 +30,10 @@ HEAD_GROUP = 4
 HEAD_GROUPS = HEADS // HEAD_GROUP
 GROUP_COLS = HEAD_GROUP * HEAD_DIM
 
+TILES = COL_BLOCKS * HEADS
+LOOKAHEAD = 8
+FINISH_LAG = 4
+
 FLOPS = 2 * ROWS * COLS * WIDTH * WIDTH + 2 * HEADS * COLS * COLS * ROWS * HEAD_DIM
 
 
@@ -47,9 +51,8 @@ def tile_rowselfattention_pa_kernel(tc, x, Wq, bq, k, out):
         keep = stack.enter_context(tc.tile_pool(name="keep", bufs=1))
         grouped_pool = stack.enter_context(tc.tile_pool(name="grouped", bufs=4))
         soft = stack.enter_context(tc.tile_pool(name="soft", bufs=8))
-        psum_t = stack.enter_context(tc.psum_pool(name="psum_t", bufs=2))
-        psum_q = stack.enter_context(tc.psum_pool(name="psum_q", bufs=3))
-        psum_s = stack.enter_context(tc.psum_pool(name="psum_s", bufs=3))
+        psum = stack.enter_context(tc.psum_pool(name="psum", bufs=8))
+        stack.enter_context(tc.manual_schedule())
 
         ident_f32 = const.tile([P, P], F32)
         make_identity(nc, ident_f32[:])
@@ -78,202 +81,226 @@ def tile_rowselfattention_pa_kernel(tc, x, Wq, bq, k, out):
             )
             return raw_tile
 
+        w_raw = [load_weight_rows(g) for g in range(PASSES)]
         x_raw = [load_columns(x_rows, 0)]
         nc.sync.dma_start(out=bias_rows[0:HEADS, :], in_=bq.rearrange("(h d) -> h d", d=HEAD_DIM))
-        w_raw = [load_weight_rows(g) for g in range(PASSES)]
-        k_raw = [load_columns(k_rows, block) for block in range(COL_BLOCKS)]
         x_raw.extend([load_columns(x_rows, block) for block in range(1, COL_BLOCKS)])
+        k_raw = [load_columns(k_rows, block) for block in range(COL_BLOCKS)]
 
-        x_codes = []
-        x_scales = []
-
-        def prepare_x(block):
-            words_in = x_raw[block][:].bitcast(F32)
-            codes = keep.tile([P, PASSES, COLS], U32, tag="x_codes", bufs=COL_BLOCKS, align_bytes=64)
-            scales = keep.tile([P, PASSES, COLS], U8, tag="x_scales", bufs=COL_BLOCKS, align_bytes=64)
-            for g in range(PASSES):
-                grouped = grouped_pool.tile([P, COLS, PACK], BF16, tag="grouped", align_bytes=64)
-                grouped_words = grouped[:].bitcast(F32)
-                for half in range(2):
-                    bank = psum_t.tile([P, 2, 2, P], F32, tag="t")
-                    for s in range(2):
-                        for u in range(2):
-                            first = (2 * g + u) * P
-                            nc.tensor.transpose(
-                                bank[:, s, u, :],
-                                words_in[:, 2 * half + s, first : first + P],
-                                ident_f32[:],
-                            )
-                    target = grouped_words[:, half * 2 * P : (half + 1) * 2 * P, :]
-                    target = target.rearrange("p (s c) u -> p s c u", s=2)
-                    source = bank[:].rearrange("p s u c -> p s c u")
-                    if half == 0:
-                        nc.vector.tensor_copy(out=target, in_=source)
-                    else:
-                        nc.scalar.copy(out=target, in_=source)
-                nc.vector.quantize_mx(
-                    out=codes[:, g, :].bitcast(FP8X4),
-                    scales=scales[:, g, :],
-                    in_=grouped[:].rearrange("p c t -> p (c t)"),
-                )
-            x_codes.append(codes)
-            x_scales.append(scales)
+        banks = {}
+        staged = {}
 
         w_codes = []
         w_scales = []
-
-        def prepare_weights(group):
-            codes = keep.tile([P, PASSES, GROUP_COLS], U32, tag="w_codes", bufs=HEAD_GROUPS, align_bytes=64)
-            scales = keep.tile([P, PASSES, GROUP_COLS], U8, tag="w_scales", bufs=HEAD_GROUPS, align_bytes=64)
-            for g in range(PASSES):
-                four_rows = w_raw[g][:].rearrange("p u (v c) -> p (u v) c", v=2)
-                four_rows = four_rows[:, :, group * GROUP_COLS : (group + 1) * GROUP_COLS]
-                grouped = grouped_pool.tile([P, GROUP_COLS, PACK], BF16, tag="grouped", align_bytes=64)
-                if group == 0:
-                    nc.vector.tensor_copy(out=grouped[:], in_=four_rows.rearrange("p t c -> p c t"))
-                else:
-                    nc.scalar.copy(out=grouped[:], in_=four_rows.rearrange("p t c -> p c t"))
-                nc.vector.quantize_mx(
-                    out=codes[:, g, :].bitcast(FP8X4),
-                    scales=scales[:, g, :],
-                    in_=grouped[:].rearrange("p c t -> p (c t)"),
-                )
-            w_codes.append(codes)
-            w_scales.append(scales)
-
-        q_codes = []
-        q_scales = []
-
-        def project(block):
-            block_codes = []
-            block_scales = []
-            for group in range(HEAD_GROUPS):
-                q_grouped = grouped_pool.tile([P, HEAD_GROUP, COLS], BF16, tag="grouped", align_bytes=64)
-                for member in range(HEAD_GROUP):
-                    h = group * HEAD_GROUP + member
-                    head_cols = slice(member * HEAD_DIM, (member + 1) * HEAD_DIM)
-                    acc = psum_q.tile([P, COLS], F32, tag="acc")
-                    for g in range(PASSES):
-                        nc.tensor.matmul_mx(
-                            out=acc[:],
-                            lhsT=w_codes[group][:, g, head_cols].bitcast(FP8X4),
-                            lhsT_scale=w_scales[group][:, g, head_cols],
-                            rhs=x_codes[block][:, g, :].bitcast(FP8X4),
-                            rhs_scale=x_scales[block][:, g, :],
-                            start=(g == 0),
-                            stop=(g == PASSES - 1),
-                        )
-                    if h % 2 == 0:
-                        nc.scalar.activation(
-                            out=q_grouped[:, member, :],
-                            in_=acc[:],
-                            func=ACT.Identity,
-                            bias=bias_scaled[:, h : h + 1],
-                            scale=factor,
-                        )
-                    else:
-                        nc.vector.tensor_scalar(
-                            out=q_grouped[:, member, :],
-                            in0=acc[:],
-                            scalar1=factor,
-                            scalar2=bias_scaled[:, h : h + 1],
-                            op0=ALU.mult,
-                            op1=ALU.add,
-                        )
-                codes = keep.tile([P, HEAD_GROUP * P], U32, tag="q_codes", bufs=COL_BLOCKS * HEAD_GROUPS, align_bytes=64)
-                scales = keep.tile([P, HEAD_GROUP * P], U8, tag="q_scales", bufs=COL_BLOCKS * HEAD_GROUPS, align_bytes=64)
-                nc.vector.quantize_mx(
-                    out=codes[:].bitcast(FP8X4),
-                    scales=scales[:],
-                    in_=q_grouped[:].rearrange("p h c -> p (h c)"),
-                )
-                block_codes.append(codes)
-                block_scales.append(scales)
-            q_codes.append(block_codes)
-            q_scales.append(block_scales)
-
-        k_codes = [
-            keep.tile([P, COLS], U32, tag="k_codes", bufs=HEADS, align_bytes=64, name="k_codes%d" % h)
-            for h in range(HEADS)
-        ]
-        k_scales = [
-            keep.tile([P, COLS], U8, tag="k_scales", bufs=HEADS, align_bytes=64, name="k_scales%d" % h)
-            for h in range(HEADS)
-        ]
-
-        def prepare_k(block):
-            word_cols = slice(block * P, (block + 1) * P)
-            for pair in range(HEADS // 2):
-                bank = psum_t.tile([P, 2, SUBS, P], BF16, tag="t")
-                for member in range(2):
-                    h = 2 * pair + member
-                    for s in range(SUBS):
-                        nc.tensor.transpose(
-                            bank[:, member, s, :],
-                            k_raw[block][:, s, h * HEAD_DIM : (h + 1) * HEAD_DIM],
-                            ident_bf16[:],
-                        )
-                k_grouped = grouped_pool.tile([P, 2, PACK * P], BF16, tag="k_grouped", align_bytes=64)
-                nc.scalar.copy(out=k_grouped[:], in_=bank[:].rearrange("p h s c -> p h (s c)"))
-                for member in range(2):
-                    h = 2 * pair + member
-                    nc.vector.quantize_mx(
-                        out=k_codes[h][:, word_cols].bitcast(FP8X4),
-                        scales=k_scales[h][:, word_cols],
-                        in_=k_grouped[:, member, :],
-                    )
-
-        def attend(block):
-            for h in range(HEADS):
-                group = h // HEAD_GROUP
-                member = h % HEAD_GROUP
-                head_words = slice(member * P, (member + 1) * P)
-                scores = psum_s.tile([P, COLS], F32, tag="scores")
-                nc.tensor.matmul_mx(
-                    out=scores[:],
-                    lhsT=q_codes[block][group][:, head_words].bitcast(FP8X4),
-                    lhsT_scale=q_scales[block][group][:, head_words],
-                    rhs=k_codes[h][:].bitcast(FP8X4),
-                    rhs_scale=k_scales[h][:],
-                    start=True,
-                    stop=True,
-                )
-                neg_max = soft.tile([P, 1], F32, tag="neg_max")
-                nc.vector.tensor_reduce(out=neg_max[:], in_=scores[:], axis=AXIS.X, op=ALU.max, negate=True)
-                weights = soft.tile([P, COLS], F32, tag="weights")
-                total = soft.tile([P, 1], F32, tag="total")
-                nc.scalar.activation(
-                    out=weights[:],
-                    in_=scores[:],
-                    func=ACT.Exp,
-                    bias=neg_max[:, 0:1],
-                    scale=1.0,
-                    accum_out=total[:],
-                )
-                inverse = soft.tile([P, 1], F32, tag="inverse")
-                nc.vector.reciprocal(out=inverse[:], in_=total[:])
-                nc.gpsimd.tensor_scalar(
-                    out=weights[:],
-                    in0=weights[:],
-                    scalar1=inverse[:, 0:1],
-                    scalar2=0.0,
-                    op0=ALU.mult,
-                    op1=ALU.add,
-                )
-                nc.sync.dma_start(out=out_rows[h, block * P : (block + 1) * P, :], in_=weights[:])
-
-        prepare_x(0)
         for group in range(HEAD_GROUPS):
-            prepare_weights(group)
-        bias_bank = psum_t.tile([P, P], BF16, tag="t")
+            w_codes.append(keep.tile([P, PASSES, GROUP_COLS], U32, tag="w_codes", bufs=HEAD_GROUPS, align_bytes=64, name="w_codes%d" % group))
+            w_scales.append(keep.tile([P, PASSES, GROUP_COLS], U8, tag="w_scales", bufs=HEAD_GROUPS, align_bytes=64, name="w_scales%d" % group))
+
+        def w_regroup(g, group):
+            four_rows = w_raw[g][:].rearrange("p u (v c) -> p (u v) c", v=2)
+            four_rows = four_rows[:, :, group * GROUP_COLS : (group + 1) * GROUP_COLS]
+            grouped = grouped_pool.tile([P, GROUP_COLS, PACK], BF16, tag="w_grouped", align_bytes=64)
+            if group == 0:
+                nc.vector.tensor_copy(out=grouped[:], in_=four_rows.rearrange("p t c -> p c t"))
+            else:
+                nc.scalar.copy(out=grouped[:], in_=four_rows.rearrange("p t c -> p c t"))
+            staged["w", g, group] = grouped
+
+        def w_quantise(g, group):
+            nc.vector.quantize_mx(
+                out=w_codes[group][:, g, :].bitcast(FP8X4),
+                scales=w_scales[group][:, g, :],
+                in_=staged["w", g, group][:].rearrange("p c t -> p (c t)"),
+            )
+
+        x_codes = []
+        x_scales = []
+        for block in range(COL_BLOCKS):
+            x_codes.append(keep.tile([P, PASSES, COLS], U32, tag="x_codes", bufs=COL_BLOCKS, align_bytes=64, name="x_codes%d" % block))
+            x_scales.append(keep.tile([P, PASSES, COLS], U8, tag="x_scales", bufs=COL_BLOCKS, align_bytes=64, name="x_scales%d" % block))
+
+        def x_transpose(u):
+            block, g, half = u // 4, (u // 2) % 2, u % 2
+            words_in = x_raw[block][:].bitcast(F32)
+            bank = psum.tile([P, 2, 2, P], F32, tag="bank")
+            for s in range(2):
+                for plane in range(2):
+                    first = (2 * g + plane) * P
+                    nc.tensor.transpose(bank[:, s, plane, :], words_in[:, 2 * half + s, first : first + P], ident_f32[:])
+            banks["x", u] = bank
+
+        def x_copy(u):
+            grouped = grouped_pool.tile([P, 2 * P, PACK], BF16, tag="x_grouped", align_bytes=64)
+            target = grouped[:].bitcast(F32).rearrange("p (s c) u -> p s c u", s=2)
+            source = banks["x", u][:].rearrange("p s u c -> p s c u")
+            if u % 2 == 0:
+                nc.vector.tensor_copy(out=target, in_=source)
+            else:
+                nc.scalar.copy(out=target, in_=source)
+            staged["x", u] = grouped
+
+        def x_quantise(u):
+            block, g, half = u // 4, (u // 2) % 2, u % 2
+            cols = slice(half * 2 * P, (half + 1) * 2 * P)
+            nc.vector.quantize_mx(
+                out=x_codes[block][:, g, cols].bitcast(FP8X4),
+                scales=x_scales[block][:, g, cols],
+                in_=staged["x", u][:].rearrange("p c t -> p (c t)"),
+            )
+
+        def x_stages(u, first, last):
+            if first <= u - 2 < last:
+                x_quantise(u - 2)
+            if first <= u - 1 < last:
+                x_copy(u - 1)
+            if first <= u < last:
+                x_transpose(u)
+
+        k_codes = []
+        k_scales = []
+        for h in range(HEADS):
+            k_codes.append(keep.tile([P, COLS], U32, tag="k_codes", bufs=HEADS, align_bytes=64, name="k_codes%d" % h))
+            k_scales.append(keep.tile([P, COLS], U8, tag="k_scales", bufs=HEADS, align_bytes=64, name="k_scales%d" % h))
+
+        def k_transpose(u):
+            block, pair = u // 4, u % 4
+            bank = psum.tile([P, 2, SUBS, P], BF16, tag="bank")
+            for member in range(2):
+                h = 2 * pair + member
+                for s in range(SUBS):
+                    nc.tensor.transpose(bank[:, member, s, :], k_raw[block][:, s, h * HEAD_DIM : (h + 1) * HEAD_DIM], ident_bf16[:])
+            banks["k", u] = bank
+
+        def k_copy(u):
+            k_grouped = grouped_pool.tile([P, 2, PACK * P], BF16, tag="k_grouped", align_bytes=64)
+            nc.scalar.copy(out=k_grouped[:], in_=banks["k", u][:].rearrange("p h s c -> p h (s c)"))
+            staged["k", u] = k_grouped
+
+        def k_quantise(u):
+            block, pair = u // 4, u % 4
+            word_cols = slice(block * P, (block + 1) * P)
+            for member in range(2):
+                h = 2 * pair + member
+                nc.vector.quantize_mx(
+                    out=k_codes[h][:, word_cols].bitcast(FP8X4),
+                    scales=k_scales[h][:, word_cols],
+                    in_=staged["k", u][:, member, :],
+                )
+
+        def k_stages(u, first, last):
+            if first <= u - 2 < last:
+                k_quantise(u - 2)
+            if first <= u - 1 < last:
+                k_copy(u - 1)
+            if first <= u < last:
+                k_transpose(u)
+
+        q_codes = {}
+        q_scales = {}
+
+        def project(n):
+            block, h = n // HEADS, n % HEADS
+            group, member = h // HEAD_GROUP, h % HEAD_GROUP
+            head_cols = slice(member * HEAD_DIM, (member + 1) * HEAD_DIM)
+            acc = psum.tile([P, COLS], F32, tag="bank")
+            for g in range(PASSES):
+                nc.tensor.matmul_mx(
+                    out=acc[:],
+                    lhsT=w_codes[group][:, g, head_cols].bitcast(FP8X4),
+                    lhsT_scale=w_scales[group][:, g, head_cols],
+                    rhs=x_codes[block][:, g, :].bitcast(FP8X4),
+                    rhs_scale=x_scales[block][:, g, :],
+                    start=(g == 0),
+                    stop=(g == PASSES - 1),
+                )
+            banks["q", n] = acc
+
+        def q_copy(n):
+            h = n % HEADS
+            q_grouped = grouped_pool.tile([P, COLS], BF16, tag="q_grouped", align_bytes=64)
+            if h % 2 == 0:
+                nc.scalar.activation(out=q_grouped[:], in_=banks["q", n][:], func=ACT.Identity, bias=bias_scaled[:, h : h + 1], scale=factor)
+            else:
+                nc.vector.tensor_scalar(out=q_grouped[:], in0=banks["q", n][:], scalar1=factor, scalar2=bias_scaled[:, h : h + 1], op0=ALU.mult, op1=ALU.add)
+            staged["q", n] = q_grouped
+
+        def q_quantise(n):
+            codes = keep.tile([P, P], U32, tag="q_codes", bufs=TILES, align_bytes=64)
+            scales = keep.tile([P, P], U8, tag="q_scales", bufs=TILES, align_bytes=64)
+            nc.vector.quantize_mx(out=codes[:].bitcast(FP8X4), scales=scales[:], in_=staged["q", n][:])
+            q_codes[n] = codes
+            q_scales[n] = scales
+
+        def q_stages(n, first, last):
+            if first <= n - 2 < last:
+                q_quantise(n - 2)
+            if first <= n - 1 < last:
+                q_copy(n - 1)
+            if first <= n < last:
+                project(n)
+
+        def scores(n):
+            h = n % HEADS
+            bank = psum.tile([P, COLS], F32, tag="bank")
+            nc.tensor.matmul_mx(
+                out=bank[:],
+                lhsT=q_codes[n][:].bitcast(FP8X4),
+                lhsT_scale=q_scales[n][:],
+                rhs=k_codes[h][:].bitcast(FP8X4),
+                rhs_scale=k_scales[h][:],
+                start=True,
+                stop=True,
+            )
+            banks["s", n] = bank
+
+        def row_max(n):
+            neg_max = soft.tile([P, 1], F32, tag="neg_max")
+            nc.vector.tensor_reduce(out=neg_max[:], in_=banks["s", n][:], axis=AXIS.X, op=ALU.max, negate=True)
+            staged["neg_max", n] = neg_max
+
+        def exponent(n):
+            weights = soft.tile([P, COLS], F32, tag="weights")
+            total = soft.tile([P, 1], F32, tag="total")
+            nc.scalar.activation(out=weights[:], in_=banks["s", n][:], func=ACT.Exp, bias=staged["neg_max", n][:, 0:1], scale=1.0, accum_out=total[:])
+            staged["weights", n] = weights
+            staged["total", n] = total
+
+        def finish(n):
+            block, h = n // HEADS, n % HEADS
+            weights = staged["weights", n]
+            inverse = soft.tile([P, 1], F32, tag="inverse")
+            nc.vector.reciprocal(out=inverse[:], in_=staged["total", n][:])
+            nc.gpsimd.tensor_scalar(out=weights[:], in0=weights[:], scalar1=inverse[:, 0:1], scalar2=0.0, op0=ALU.mult, op1=ALU.add)
+            nc.sync.dma_start(out=out_rows[h, block * P : (block + 1) * P, :], in_=weights[:])
+
+        def attention_stages(n):
+            if 0 <= n - FINISH_LAG < TILES:
+                finish(n - FINISH_LAG)
+            if 0 <= n - 2 < TILES:
+                exponent(n - 2)
+            if 0 <= n - 1 < TILES:
+                row_max(n - 1)
+            if 0 <= n < TILES:
+                scores(n)
+
+        for g in range(PASSES):
+            for group in range(HEAD_GROUPS):
+                w_regroup(g, group)
+        for group in range(HEAD_GROUPS):
+            for g in range(PASSES):
+                w_quantise(g, group)
+        bias_bank = psum.tile([P, P], BF16, tag="bank")
         nc.tensor.transpose(bias_bank[:], bias_rows[:], ident_bf16[:])
         bias_scaled = const.tile([P, HEADS], F32)
         nc.vector.tensor_scalar_mul(out=bias_scaled[:], in0=bias_bank[:, 0:HEADS], scalar1=factor)
-        project(0)
-        for block in range(COL_BLOCKS):
-            prepare_k(block)
-        for block in range(COL_BLOCKS):
-            if block + 1 < COL_BLOCKS:
-                prepare_x(block + 1)
-                project(block + 1)
-            attend(block)
+        for u in range(0, 8 + 2):
+            x_stages(u, 0, 8)
+        for n in range(0, LOOKAHEAD + 2):
+            q_stages(n, 0, LOOKAHEAD)
+        for u in range(8, 16 + 2):
+            x_stages(u, 8, 16)
+        for u in range(0, 16 + 2):
+            k_stages(u, 0, 16)
+        for n in range(0, TILES + FINISH_LAG + 1):
+            q_stages(n + LOOKAHEAD, LOOKAHEAD, TILES)
+            attention_stages(n)

@@ -133,10 +133,7 @@ def tile_rowselfattention_pa_kernel(tc, x, Wq, bq, k, out):
             grouped = grouped_pool.tile([P, 2 * P, PACK], BF16, tag="x_grouped", align_bytes=64)
             target = grouped[:].bitcast(F32).rearrange("p (s c) u -> p s c u", s=2)
             source = banks["x", u][:].rearrange("p s u c -> p s c u")
-            if u % 2 == 0:
-                nc.vector.tensor_copy(out=target, in_=source)
-            else:
-                nc.scalar.copy(out=target, in_=source)
+            nc.scalar.copy(out=target, in_=source)
             staged["x", u] = grouped
 
         def x_quantise(u):
@@ -173,7 +170,11 @@ def tile_rowselfattention_pa_kernel(tc, x, Wq, bq, k, out):
 
         def k_copy(u):
             k_grouped = grouped_pool.tile([P, 2, PACK * P], BF16, tag="k_grouped", align_bytes=64)
-            nc.scalar.copy(out=k_grouped[:], in_=banks["k", u][:].rearrange("p h s c -> p h (s c)"))
+            source = banks["k", u][:].rearrange("p h s c -> p h (s c)")
+            if u % 2 == 0:
+                nc.vector.tensor_copy(out=k_grouped[:], in_=source)
+            else:
+                nc.scalar.copy(out=k_grouped[:], in_=source)
             staged["k", u] = k_grouped
 
         def k_quantise(u):

@@ -133,7 +133,10 @@ def tile_rowselfattention_pa_kernel(tc, x, Wq, bq, k, out):
             grouped = grouped_pool.tile([P, 2 * P, PACK], BF16, tag="x_grouped", align_bytes=64)
             target = grouped[:].bitcast(F32).rearrange("p (s c) u -> p s c u", s=2)
             source = banks["x", u][:].rearrange("p s u c -> p s c u")
-            nc.scalar.copy(out=target, in_=source)
+            if u % 2 == 0:
+                nc.vector.tensor_copy(out=target, in_=source)
+            else:
+                nc.scalar.copy(out=target, in_=source)
             staged["x", u] = grouped
 
         def x_quantise(u):
@@ -170,11 +173,7 @@ def tile_rowselfattention_pa_kernel(tc, x, Wq, bq, k, out):
 
         def k_copy(u):
             k_grouped = grouped_pool.tile([P, 2, PACK * P], BF16, tag="k_grouped", align_bytes=64)
-            source = banks["k", u][:].rearrange("p h s c -> p h (s c)")
-            if u % 2 == 0:
-                nc.vector.tensor_copy(out=k_grouped[:], in_=source)
-            else:
-                nc.scalar.copy(out=k_grouped[:], in_=source)
+            nc.scalar.copy(out=k_grouped[:], in_=banks["k", u][:].rearrange("p h s c -> p h (s c)"))
             staged["k", u] = k_grouped
 
         def k_quantise(u):
@@ -219,10 +218,7 @@ def tile_rowselfattention_pa_kernel(tc, x, Wq, bq, k, out):
         def q_copy(n):
             h = n % HEADS
             q_grouped = grouped_pool.tile([P, COLS], BF16, tag="q_grouped", align_bytes=64)
-            if h % 2 == 0:
-                nc.scalar.activation(out=q_grouped[:], in_=banks["q", n][:], func=ACT.Identity, bias=bias_scaled[:, h : h + 1], scale=factor)
-            else:
-                nc.vector.tensor_scalar(out=q_grouped[:], in0=banks["q", n][:], scalar1=factor, scalar2=bias_scaled[:, h : h + 1], op0=ALU.mult, op1=ALU.add)
+            nc.scalar.activation(out=q_grouped[:], in_=banks["q", n][:], func=ACT.Identity, bias=bias_scaled[:, h : h + 1], scale=factor)
             staged["q", n] = q_grouped
 
         def q_quantise(n):
@@ -271,7 +267,7 @@ def tile_rowselfattention_pa_kernel(tc, x, Wq, bq, k, out):
             weights = staged["weights", n]
             inverse = soft.tile([P, 1], F32, tag="inverse")
             nc.vector.reciprocal(out=inverse[:], in_=staged["total", n][:])
-            nc.gpsimd.tensor_scalar(out=weights[:], in0=weights[:], scalar1=inverse[:, 0:1], scalar2=0.0, op0=ALU.mult, op1=ALU.add)
+            nc.vector.tensor_scalar_mul(out=weights[:], in0=weights[:], scalar1=inverse[:, 0:1])
             nc.sync.dma_start(out=out_rows[h, block * P : (block + 1) * P, :], in_=weights[:])
 
         def attention_stages(n):

@@ -29,10 +29,13 @@ SUBS = P // SUB
 HEAD_GROUP = 4
 HEAD_GROUPS = HEADS // HEAD_GROUP
 GROUP_COLS = HEAD_GROUP * HEAD_DIM
+HEAD_PAIRS = HEADS // 2
+K_BANKS = COL_BLOCKS * HEAD_PAIRS
 
-TILES = COL_BLOCKS * HEADS
-LOOKAHEAD = 8
-FINISH_LAG = 4
+PIECES = COL_BLOCKS * HEADS
+LOOKAHEAD = 4
+PREPARE_STAGES = 3
+SOFTMAX_STAGES = 6
 
 FLOPS = 2 * ROWS * COLS * WIDTH * WIDTH + 2 * HEADS * COLS * COLS * ROWS * HEAD_DIM
 
@@ -84,8 +87,8 @@ def tile_rowselfattention_pa_kernel(tc, x, Wq, bq, k, out):
         w_raw = [load_weight_rows(g) for g in range(PASSES)]
         x_raw = [load_columns(x_rows, 0)]
         nc.sync.dma_start(out=bias_rows[0:HEADS, :], in_=bq.rearrange("(h d) -> h d", d=HEAD_DIM))
-        x_raw.extend([load_columns(x_rows, block) for block in range(1, COL_BLOCKS)])
         k_raw = [load_columns(k_rows, block) for block in range(COL_BLOCKS)]
+        x_raw.extend([load_columns(x_rows, block) for block in range(1, COL_BLOCKS)])
 
         banks = {}
         staged = {}
@@ -119,42 +122,39 @@ def tile_rowselfattention_pa_kernel(tc, x, Wq, bq, k, out):
             x_codes.append(keep.tile([P, PASSES, COLS], U32, tag="x_codes", bufs=COL_BLOCKS, align_bytes=64, name="x_codes%d" % block))
             x_scales.append(keep.tile([P, PASSES, COLS], U8, tag="x_scales", bufs=COL_BLOCKS, align_bytes=64, name="x_scales%d" % block))
 
-        def x_transpose(u):
-            block, g, half = u // 4, (u // 2) % 2, u % 2
+        def x_transpose(v):
+            block, g = v // PASSES, v % PASSES
             words_in = x_raw[block][:].bitcast(F32)
-            bank = psum.tile([P, 2, 2, P], F32, tag="bank")
-            for s in range(2):
-                for plane in range(2):
-                    first = (2 * g + plane) * P
-                    nc.tensor.transpose(bank[:, s, plane, :], words_in[:, 2 * half + s, first : first + P], ident_f32[:])
-            banks["x", u] = bank
+            for half in range(2):
+                bank = psum.tile([P, 2, 2, P], F32, tag="bank")
+                for s in range(2):
+                    for u in range(2):
+                        plane = slice((2 * g + u) * P, (2 * g + u + 1) * P)
+                        nc.tensor.transpose(bank[:, s, u, :], words_in[:, 2 * half + s, plane], ident_f32[:])
+                banks["x", v, half] = bank
 
-        def x_copy(u):
-            grouped = grouped_pool.tile([P, 2 * P, PACK], BF16, tag="x_grouped", align_bytes=64)
-            target = grouped[:].bitcast(F32).rearrange("p (s c) u -> p s c u", s=2)
-            source = banks["x", u][:].rearrange("p s u c -> p s c u")
-            if u % 2 == 0:
-                nc.vector.tensor_copy(out=target, in_=source)
-            else:
-                nc.scalar.copy(out=target, in_=source)
-            staged["x", u] = grouped
+        def x_copy(v):
+            grouped = grouped_pool.tile([P, COLS, PACK], BF16, tag="x_grouped", align_bytes=64)
+            grouped_words = grouped[:].bitcast(F32).rearrange("p (half s c) u -> p half s c u", half=2, s=2)
+            nc.vector.tensor_copy(out=grouped_words[:, 0], in_=banks["x", v, 0][:].rearrange("p s u c -> p s c u"))
+            nc.scalar.copy(out=grouped_words[:, 1], in_=banks["x", v, 1][:].rearrange("p s u c -> p s c u"))
+            staged["x", v] = grouped
 
-        def x_quantise(u):
-            block, g, half = u // 4, (u // 2) % 2, u % 2
-            cols = slice(half * 2 * P, (half + 1) * 2 * P)
+        def x_quantise(v):
+            block, g = v // PASSES, v % PASSES
             nc.vector.quantize_mx(
-                out=x_codes[block][:, g, cols].bitcast(FP8X4),
-                scales=x_scales[block][:, g, cols],
-                in_=staged["x", u][:].rearrange("p c t -> p (c t)"),
+                out=x_codes[block][:, g, :].bitcast(FP8X4),
+                scales=x_scales[block][:, g, :],
+                in_=staged["x", v][:].rearrange("p c t -> p (c t)"),
             )
 
-        def x_stages(u, first, last):
-            if first <= u - 2 < last:
-                x_quantise(u - 2)
-            if first <= u - 1 < last:
-                x_copy(u - 1)
-            if first <= u < last:
-                x_transpose(u)
+        def x_stages(v, first, last):
+            if first <= v - 1 < last:
+                x_copy(v - 1)
+            if first <= v - 2 < last:
+                x_quantise(v - 2)
+            if first <= v < last:
+                x_transpose(v)
 
         k_codes = []
         k_scales = []
@@ -162,38 +162,38 @@ def tile_rowselfattention_pa_kernel(tc, x, Wq, bq, k, out):
             k_codes.append(keep.tile([P, COLS], U32, tag="k_codes", bufs=HEADS, align_bytes=64, name="k_codes%d" % h))
             k_scales.append(keep.tile([P, COLS], U8, tag="k_scales", bufs=HEADS, align_bytes=64, name="k_scales%d" % h))
 
-        def k_transpose(u):
-            block, pair = u // 4, u % 4
+        def k_transpose(bank_no):
+            block, pair = bank_no // HEAD_PAIRS, bank_no % HEAD_PAIRS
             bank = psum.tile([P, 2, SUBS, P], BF16, tag="bank")
             for member in range(2):
                 h = 2 * pair + member
                 for s in range(SUBS):
                     nc.tensor.transpose(bank[:, member, s, :], k_raw[block][:, s, h * HEAD_DIM : (h + 1) * HEAD_DIM], ident_bf16[:])
-            banks["k", u] = bank
+            banks["k", bank_no] = bank
 
-        def k_copy(u):
+        def k_copy(bank_no):
             k_grouped = grouped_pool.tile([P, 2, PACK * P], BF16, tag="k_grouped", align_bytes=64)
-            nc.scalar.copy(out=k_grouped[:], in_=banks["k", u][:].rearrange("p h s c -> p h (s c)"))
-            staged["k", u] = k_grouped
+            nc.scalar.copy(out=k_grouped[:], in_=banks["k", bank_no][:].rearrange("p h s c -> p h (s c)"))
+            staged["k", bank_no] = k_grouped
 
-        def k_quantise(u):
-            block, pair = u // 4, u % 4
+        def k_quantise(bank_no):
+            block, pair = bank_no // HEAD_PAIRS, bank_no % HEAD_PAIRS
             word_cols = slice(block * P, (block + 1) * P)
             for member in range(2):
                 h = 2 * pair + member
                 nc.vector.quantize_mx(
                     out=k_codes[h][:, word_cols].bitcast(FP8X4),
                     scales=k_scales[h][:, word_cols],
-                    in_=staged["k", u][:, member, :],
+                    in_=staged["k", bank_no][:, member, :],
                 )
 
-        def k_stages(u, first, last):
-            if first <= u - 2 < last:
-                k_quantise(u - 2)
-            if first <= u - 1 < last:
-                k_copy(u - 1)
-            if first <= u < last:
-                k_transpose(u)
+        def k_stages(bank_no, first, last):
+            if first <= bank_no - 1 < last:
+                k_copy(bank_no - 1)
+            if first <= bank_no - 2 < last:
+                k_quantise(bank_no - 2)
+            if first <= bank_no < last:
+                k_transpose(bank_no)
 
         q_codes = {}
         q_scales = {}
@@ -222,17 +222,17 @@ def tile_rowselfattention_pa_kernel(tc, x, Wq, bq, k, out):
             staged["q", n] = q_grouped
 
         def q_quantise(n):
-            codes = keep.tile([P, P], U32, tag="q_codes", bufs=TILES, align_bytes=64)
-            scales = keep.tile([P, P], U8, tag="q_scales", bufs=TILES, align_bytes=64)
+            codes = keep.tile([P, P], U32, tag="q_codes", bufs=PIECES, align_bytes=64)
+            scales = keep.tile([P, P], U8, tag="q_scales", bufs=PIECES, align_bytes=64)
             nc.vector.quantize_mx(out=codes[:].bitcast(FP8X4), scales=scales[:], in_=staged["q", n][:])
             q_codes[n] = codes
             q_scales[n] = scales
 
         def q_stages(n, first, last):
-            if first <= n - 2 < last:
-                q_quantise(n - 2)
             if first <= n - 1 < last:
                 q_copy(n - 1)
+            if first <= n - 2 < last:
+                q_quantise(n - 2)
             if first <= n < last:
                 project(n)
 
@@ -262,22 +262,27 @@ def tile_rowselfattention_pa_kernel(tc, x, Wq, bq, k, out):
             staged["weights", n] = weights
             staged["total", n] = total
 
-        def finish(n):
-            block, h = n // HEADS, n % HEADS
-            weights = staged["weights", n]
+        def invert(n):
             inverse = soft.tile([P, 1], F32, tag="inverse")
             nc.vector.reciprocal(out=inverse[:], in_=staged["total", n][:])
-            nc.vector.tensor_scalar_mul(out=weights[:], in0=weights[:], scalar1=inverse[:, 0:1])
+            staged["inverse", n] = inverse
+
+        def normalise(n):
+            block, h = n // HEADS, n % HEADS
+            weights = staged["weights", n]
+            nc.vector.tensor_scalar_mul(out=weights[:], in0=weights[:], scalar1=staged["inverse", n][:, 0:1])
             nc.sync.dma_start(out=out_rows[h, block * P : (block + 1) * P, :], in_=weights[:])
 
-        def attention_stages(n):
-            if 0 <= n - FINISH_LAG < TILES:
-                finish(n - FINISH_LAG)
-            if 0 <= n - 2 < TILES:
+        def softmax_stages(n):
+            if 0 <= n - 5 < PIECES:
+                normalise(n - 5)
+            if 0 <= n - 4 < PIECES:
+                invert(n - 4)
+            if 0 <= n - 2 < PIECES:
                 exponent(n - 2)
-            if 0 <= n - 1 < TILES:
+            if 0 <= n - 1 < PIECES:
                 row_max(n - 1)
-            if 0 <= n < TILES:
+            if 0 <= n < PIECES:
                 scores(n)
 
         for g in range(PASSES):
@@ -290,14 +295,15 @@ def tile_rowselfattention_pa_kernel(tc, x, Wq, bq, k, out):
         nc.tensor.transpose(bias_bank[:], bias_rows[:], ident_bf16[:])
         bias_scaled = const.tile([P, HEADS], F32)
         nc.vector.tensor_scalar_mul(out=bias_scaled[:], in0=bias_bank[:, 0:HEADS], scalar1=factor)
-        for u in range(0, 8 + 2):
-            x_stages(u, 0, 8)
-        for n in range(0, LOOKAHEAD + 2):
+        for v in range(PASSES + PREPARE_STAGES - 1):
+            x_stages(v, 0, PASSES)
+        for n in range(LOOKAHEAD + PREPARE_STAGES - 1):
             q_stages(n, 0, LOOKAHEAD)
-        for u in range(8, 16 + 2):
-            x_stages(u, 8, 16)
-        for u in range(0, 16 + 2):
-            k_stages(u, 0, 16)
-        for n in range(0, TILES + FINISH_LAG + 1):
-            q_stages(n + LOOKAHEAD, LOOKAHEAD, TILES)
-            attention_stages(n)
+        for bank_no in range(K_BANKS + PREPARE_STAGES - 1):
+            k_stages(bank_no, 0, K_BANKS)
+        for n in range(PIECES + SOFTMAX_STAGES - 1):
+            block, h = n // HEADS, n % HEADS
+            if block + 1 < COL_BLOCKS and h < PASSES + PREPARE_STAGES - 1:
+                x_stages(PASSES * (block + 1) + h, PASSES * (block + 1), PASSES * (block + 2))
+            q_stages(n + LOOKAHEAD, LOOKAHEAD, PIECES)
+            softmax_stages(n)

@@ -33,7 +33,7 @@ HEAD_PAIRS = HEADS // 2
 K_BANKS = COL_BLOCKS * HEAD_PAIRS
 
 PIECES = COL_BLOCKS * HEADS
-LOOKAHEAD = 4
+LOOKAHEAD = 3
 PREPARE_STAGES = 3
 SOFTMAX_STAGES = 6
 
@@ -84,8 +84,8 @@ def tile_rowselfattention_pa_kernel(tc, x, Wq, bq, k, out):
             )
             return raw_tile
 
-        w_raw = [load_weight_rows(g) for g in range(PASSES)]
         x_raw = [load_columns(x_rows, 0)]
+        w_raw = [load_weight_rows(g) for g in range(PASSES)]
         nc.sync.dma_start(out=bias_rows[0:HEADS, :], in_=bq.rearrange("(h d) -> h d", d=HEAD_DIM))
         k_raw = [load_columns(k_rows, block) for block in range(COL_BLOCKS)]
         x_raw.extend([load_columns(x_rows, block) for block in range(1, COL_BLOCKS)])
@@ -285,6 +285,8 @@ def tile_rowselfattention_pa_kernel(tc, x, Wq, bq, k, out):
             if 0 <= n < PIECES:
                 scores(n)
 
+        for v in range(PASSES + PREPARE_STAGES - 1):
+            x_stages(v, 0, PASSES)
         for g in range(PASSES):
             for group in range(HEAD_GROUPS):
                 w_regroup(g, group)
@@ -295,8 +297,6 @@ def tile_rowselfattention_pa_kernel(tc, x, Wq, bq, k, out):
         nc.tensor.transpose(bias_bank[:], bias_rows[:], ident_bf16[:])
         bias_scaled = const.tile([P, HEADS], F32)
         nc.vector.tensor_scalar_mul(out=bias_scaled[:], in0=bias_bank[:, 0:HEADS], scalar1=factor)
-        for v in range(PASSES + PREPARE_STAGES - 1):
-            x_stages(v, 0, PASSES)
         for n in range(LOOKAHEAD + PREPARE_STAGES - 1):
             q_stages(n, 0, LOOKAHEAD)
         for bank_no in range(K_BANKS + PREPARE_STAGES - 1):

@@ -36,6 +36,8 @@ PIECES = COL_BLOCKS * HEADS
 LOOKAHEAD = 3
 PREPARE_STAGES = 3
 SOFTMAX_STAGES = 6
+WARM_FIRST = 8
+WARM_SECOND = 4
 
 FLOPS = 2 * ROWS * COLS * WIDTH * WIDTH + 2 * HEADS * COLS * COLS * ROWS * HEAD_DIM
 
@@ -66,6 +68,8 @@ def tile_rowselfattention_pa_kernel(tc, x, Wq, bq, k, out):
         nc.scalar.activation(out=warm[:], in_=warm[:], func=ACT.Exp)
         bias_rows = const.tile([P, P], BF16)
         nc.vector.memset(bias_rows[:], 0.0)
+        zero_rows = const.tile([P, COLS], BF16)
+        nc.vector.memset(zero_rows[:], 0.0)
 
         def load_columns(rows, block):
             raw_tile = raw.tile([P, SUBS, WIDTH], BF16, tag="raw")
@@ -285,11 +289,18 @@ def tile_rowselfattention_pa_kernel(tc, x, Wq, bq, k, out):
             if 0 <= n < PIECES:
                 scores(n)
 
+        def idle_matmuls(count, moving):
+            idle_bank = psum.tile([P, COLS], F32, tag="bank")
+            for i in range(count):
+                nc.tensor.matmul(out=idle_bank[:], lhsT=ident_bf16[:], rhs=moving, start=True, stop=True)
+
+        idle_matmuls(WARM_FIRST, zero_rows[:])
         for v in range(PASSES + PREPARE_STAGES - 1):
             x_stages(v, 0, PASSES)
         for g in range(PASSES):
             for group in range(HEAD_GROUPS):
                 w_regroup(g, group)
+        idle_matmuls(WARM_SECOND, staged["w", 0, 0][:, 0:P, :].rearrange("p c t -> p (c t)"))
         for group in range(HEAD_GROUPS):
             for g in range(PASSES):
                 w_quantise(g, group)

@@ -36,6 +36,7 @@ PIECES = COL_BLOCKS * HEADS
 LOOKAHEAD = 3
 PREPARE_STAGES = 3
 SOFTMAX_STAGES = 6
+K_COPY_TURN = 3
 WARM_FIRST = 8
 WARM_SECOND = 4
 
@@ -177,7 +178,10 @@ def tile_rowselfattention_pa_kernel(tc, x, Wq, bq, k, out):
 
         def k_copy(bank_no):
             k_grouped = grouped_pool.tile([P, 2, PACK * P], BF16, tag="k_grouped", align_bytes=64)
-            nc.scalar.copy(out=k_grouped[:], in_=banks["k", bank_no][:].rearrange("p h s c -> p h (s c)"))
+            if bank_no % K_COPY_TURN == 1:
+                nc.vector.tensor_copy(out=k_grouped[:], in_=banks["k", bank_no][:].rearrange("p h s c -> p h (s c)"))
+            else:
+                nc.scalar.copy(out=k_grouped[:], in_=banks["k", bank_no][:].rearrange("p h s c -> p h (s c)"))
             staged["k", bank_no] = k_grouped
 
         def k_quantise(bank_no):

@@ -35,7 +35,7 @@ K_BANKS = COL_BLOCKS * HEAD_PAIRS
 PIECES = COL_BLOCKS * HEADS
 LOOKAHEAD = 3
 PREPARE_STAGES = 3
-SOFTMAX_STAGES = 6
+SOFTMAX_STAGES = 5
 K_COPY_TURN = 3
 WARM_FIRST = 8
 WARM_SECOND = 4
@@ -282,10 +282,10 @@ def tile_rowselfattention_pa_kernel(tc, x, Wq, bq, k, out):
             nc.sync.dma_start(out=out_rows[h, block * P : (block + 1) * P, :], in_=weights[:])
 
         def softmax_stages(n):
-            if 0 <= n - 5 < PIECES:
-                normalise(n - 5)
             if 0 <= n - 4 < PIECES:
-                invert(n - 4)
+                normalise(n - 4)
+            if 0 <= n - 3 < PIECES:
+                invert(n - 3)
             if 0 <= n - 2 < PIECES:
                 exponent(n - 2)
             if 0 <= n - 1 < PIECES:

import math
from contextlib import ExitStack

import concourse.mybir as mybir
from concourse.masks import make_identity

F32 = mybir.dt.float32
BF16 = mybir.dt.bfloat16
U32 = mybir.dt.uint32
U8 = mybir.dt.uint8
FP8X4 = mybir.dt.float8_e4m3fn_x4
ACT = mybir.ActivationFunctionType
ALU = mybir.AluOpType
AXIS = mybir.AxisListType

P = 128
PACK = 4
K_PASS = P * PACK

ROWS = 4
COLS = 512
WIDTH = 1024
HEADS = 8
HEAD_DIM = WIDTH // HEADS
PASSES = WIDTH // K_PASS
COL_BLOCKS = COLS // P
SUB = P // ROWS
SUBS = P // SUB
HEAD_GROUP = 4
HEAD_GROUPS = HEADS // HEAD_GROUP
GROUP_COLS = HEAD_GROUP * HEAD_DIM
HEAD_PAIRS = HEADS // 2
K_BANKS = COL_BLOCKS * HEAD_PAIRS

PIECES = COL_BLOCKS * HEADS
LOOKAHEAD = 3
PREPARE_STAGES = 3
SOFTMAX_STAGES = 5
K_COPY_TURN = 3
WARM_FIRST = 8
WARM_SECOND = 4

FLOPS = 2 * ROWS * COLS * WIDTH * WIDTH + 2 * HEADS * COLS * COLS * ROWS * HEAD_DIM


def tile_rowselfattention_pa_kernel(tc, x, Wq, bq, k, out):
    nc = tc.nc
    factor = 1.0 / math.sqrt(HEAD_DIM * ROWS)

    x_rows = x.rearrange("r i b e -> r (i b) e")
    k_rows = k.rearrange("r j b h d -> r (j b) (h d)")
    out_rows = out.rearrange("h b i j -> h (b i) j")

    with ExitStack() as stack:
        const = stack.enter_context(tc.tile_pool(name="const", bufs=1))
        raw = stack.enter_context(tc.tile_pool(name="raw", bufs=2 * COL_BLOCKS + PASSES))
        keep = stack.enter_context(tc.tile_pool(name="keep", bufs=1))
        grouped_pool = stack.enter_context(tc.tile_pool(name="grouped", bufs=4))
        soft = stack.enter_context(tc.tile_pool(name="soft", bufs=8))
        psum = stack.enter_context(tc.psum_pool(name="psum", bufs=8))
        stack.enter_context(tc.manual_schedule())

        ident_f32 = const.tile([P, P], F32)
        make_identity(nc, ident_f32[:])
        ident_bf16 = const.tile([P, P], BF16)
        make_identity(nc, ident_bf16[:])
        warm = const.tile([P, 1], F32)
        nc.vector.memset(warm[:], 0.0)
        nc.scalar.activation(out=warm[:], in_=warm[:], func=ACT.Exp)
        bias_rows = const.tile([P, P], BF16)
        nc.vector.memset(bias_rows[:], 0.0)
        zero_rows = const.tile([P, COLS], BF16)
        nc.vector.memset(zero_rows[:], 0.0)

        def load_columns(rows, block):
            raw_tile = raw.tile([P, SUBS, WIDTH], BF16, tag="raw")
            for r in range(ROWS):
                nc.sync.dma_start(
                    out=raw_tile[r:P:ROWS, :, :],
                    in_=rows[r, block * P : (block + 1) * P, :].rearrange("(s c) e -> c s e", c=SUB),
                )
            return raw_tile

        def load_weight_rows(g):
            raw_tile = raw.tile([P, 2, 2 * WIDTH], BF16, tag="raw")
            nc.sync.dma_start(
                out=raw_tile[:],
                in_=Wq[g * K_PASS : (g + 1) * K_PASS, :].rearrange("(u p v) c -> p u (v c)", u=2, v=2),
            )
            return raw_tile

        x_raw = [load_columns(x_rows, 0)]
        w_raw = [load_weight_rows(g) for g in range(PASSES)]
        nc.sync.dma_start(out=bias_rows[0:HEADS, :], in_=bq.rearrange("(h d) -> h d", d=HEAD_DIM))
        k_raw = [load_columns(k_rows, block) for block in range(COL_BLOCKS)]
        x_raw.extend([load_columns(x_rows, block) for block in range(1, COL_BLOCKS)])

        banks = {}
        staged = {}

        w_codes = []
        w_scales = []
        for group in range(HEAD_GROUPS):
            w_codes.append(keep.tile([P, PASSES, GROUP_COLS], U32, tag="w_codes", bufs=HEAD_GROUPS, align_bytes=64, name="w_codes%d" % group))
            w_scales.append(keep.tile([P, PASSES, GROUP_COLS], U8, tag="w_scales", bufs=HEAD_GROUPS, align_bytes=64, name="w_scales%d" % group))

        def w_regroup(g, group):
            four_rows = w_raw[g][:].rearrange("p u (v c) -> p (u v) c", v=2)
            four_rows = four_rows[:, :, group * GROUP_COLS : (group + 1) * GROUP_COLS]
            grouped = grouped_pool.tile([P, GROUP_COLS, PACK], BF16, tag="w_grouped", align_bytes=64)
            if group == 0:
                nc.vector.tensor_copy(out=grouped[:], in_=four_rows.rearrange("p t c -> p c t"))
            else:
                nc.scalar.copy(out=grouped[:], in_=four_rows.rearrange("p t c -> p c t"))
            staged["w", g, group] = grouped

        def w_quantise(g, group):
            nc.vector.quantize_mx(
                out=w_codes[group][:, g, :].bitcast(FP8X4),
                scales=w_scales[group][:, g, :],
                in_=staged["w", g, group][:].rearrange("p c t -> p (c t)"),
            )

        x_codes = []
        x_scales = []
        for block in range(COL_BLOCKS):
            x_codes.append(keep.tile([P, PASSES, COLS], U32, tag="x_codes", bufs=COL_BLOCKS, align_bytes=64, name="x_codes%d" % block))
            x_scales.append(keep.tile([P, PASSES, COLS], U8, tag="x_scales", bufs=COL_BLOCKS, align_bytes=64, name="x_scales%d" % block))

        def x_transpose(v):
            block, g = v // PASSES, v % PASSES
            words_in = x_raw[block][:].bitcast(F32)
            for half in range(2):
                bank = psum.tile([P, 2, 2, P], F32, tag="bank")
                for s in range(2):
                    for u in range(2):
                        plane = slice((2 * g + u) * P, (2 * g + u + 1) * P)
                        nc.tensor.transpose(bank[:, s, u, :], words_in[:, 2 * half + s, plane], ident_f32[:])
                banks["x", v, half] = bank

        def x_copy(v):
            grouped = grouped_pool.tile([P, COLS, PACK], BF16, tag="x_grouped", align_bytes=64)
            grouped_words = grouped[:].bitcast(F32).rearrange("p (half s c) u -> p half s c u", half=2, s=2)
            nc.vector.tensor_copy(out=grouped_words[:, 0], in_=banks["x", v, 0][:].rearrange("p s u c -> p s c u"))
            nc.scalar.copy(out=grouped_words[:, 1], in_=banks["x", v, 1][:].rearrange("p s u c -> p s c u"))
            staged["x", v] = grouped

        def x_quantise(v):
            block, g = v // PASSES, v % PASSES
            nc.vector.quantize_mx(
                out=x_codes[block][:, g, :].bitcast(FP8X4),
                scales=x_scales[block][:, g, :],
                in_=staged["x", v][:].rearrange("p c t -> p (c t)"),
            )

        def x_stages(v, first, last):
            if first <= v - 1 < last:
                x_copy(v - 1)
            if first <= v - 2 < last:
                x_quantise(v - 2)
            if first <= v < last:
                x_transpose(v)

        k_codes = []
        k_scales = []
        for h in range(HEADS):
            k_codes.append(keep.tile([P, COLS], U32, tag="k_codes", bufs=HEADS, align_bytes=64, name="k_codes%d" % h))
            k_scales.append(keep.tile([P, COLS], U8, tag="k_scales", bufs=HEADS, align_bytes=64, name="k_scales%d" % h))

        def k_transpose(bank_no):
            block, pair = bank_no // HEAD_PAIRS, bank_no % HEAD_PAIRS
            bank = psum.tile([P, 2, SUBS, P], BF16, tag="bank")
            for member in range(2):
                h = 2 * pair + member
                for s in range(SUBS):
                    nc.tensor.transpose(bank[:, member, s, :], k_raw[block][:, s, h * HEAD_DIM : (h + 1) * HEAD_DIM], ident_bf16[:])
            banks["k", bank_no] = bank

        def k_copy(bank_no):
            k_grouped = grouped_pool.tile([P, 2, PACK * P], BF16, tag="k_grouped", align_bytes=64)
            if bank_no % K_COPY_TURN == 1:
                nc.vector.tensor_copy(out=k_grouped[:], in_=banks["k", bank_no][:].rearrange("p h s c -> p h (s c)"))
            else:
                nc.scalar.copy(out=k_grouped[:], in_=banks["k", bank_no][:].rearrange("p h s c -> p h (s c)"))
            staged["k", bank_no] = k_grouped

        def k_quantise(bank_no):
            block, pair = bank_no // HEAD_PAIRS, bank_no % HEAD_PAIRS
            word_cols = slice(block * P, (block + 1) * P)
            for member in range(2):
                h = 2 * pair + member
                nc.vector.quantize_mx(
                    out=k_codes[h][:, word_cols].bitcast(FP8X4),
                    scales=k_scales[h][:, word_cols],
                    in_=staged["k", bank_no][:, member, :],
                )

        def k_stages(bank_no, first, last):
            if first <= bank_no - 1 < last:
                k_copy(bank_no - 1)
            if first <= bank_no - 2 < last:
                k_quantise(bank_no - 2)
            if first <= bank_no < last:
                k_transpose(bank_no)

        q_codes = {}
        q_scales = {}

        def project(n):
            block, h = n // HEADS, n % HEADS
            group, member = h // HEAD_GROUP, h % HEAD_GROUP
            head_cols = slice(member * HEAD_DIM, (member + 1) * HEAD_DIM)
            acc = psum.tile([P, COLS], F32, tag="bank")
            for g in range(PASSES):
                nc.tensor.matmul_mx(
                    out=acc[:],
                    lhsT=w_codes[group][:, g, head_cols].bitcast(FP8X4),
                    lhsT_scale=w_scales[group][:, g, head_cols],
                    rhs=x_codes[block][:, g, :].bitcast(FP8X4),
                    rhs_scale=x_scales[block][:, g, :],
                    start=(g == 0),
                    stop=(g == PASSES - 1),
                )
            banks["q", n] = acc

        def q_copy(n):
            h = n % HEADS
            q_grouped = grouped_pool.tile([P, COLS], BF16, tag="q_grouped", align_bytes=64)
            nc.scalar.activation(out=q_grouped[:], in_=banks["q", n][:], func=ACT.Identity, bias=bias_scaled[:, h : h + 1], scale=factor)
            staged["q", n] = q_grouped

        def q_quantise(n):
            codes = keep.tile([P, P], U32, tag="q_codes", bufs=PIECES, align_bytes=64)
            scales = keep.tile([P, P], U8, tag="q_scales", bufs=PIECES, align_bytes=64)
            nc.vector.quantize_mx(out=codes[:].bitcast(FP8X4), scales=scales[:], in_=staged["q", n][:])
            q_codes[n] = codes
            q_scales[n] = scales

        def q_stages(n, first, last):
            if first <= n - 1 < last:
                q_copy(n - 1)
            if first <= n - 2 < last:
                q_quantise(n - 2)
            if first <= n < last:
                project(n)

        def scores(n):
            h = n % HEADS
            bank = psum.tile([P, COLS], F32, tag="bank")
            nc.tensor.matmul_mx(
                out=bank[:],
                lhsT=q_codes[n][:].bitcast(FP8X4),
                lhsT_scale=q_scales[n][:],
                rhs=k_codes[h][:].bitcast(FP8X4),
                rhs_scale=k_scales[h][:],
                start=True,
                stop=True,
            )
            banks["s", n] = bank

        def row_max(n):
            neg_max = soft.tile([P, 1], F32, tag="neg_max")
            nc.vector.tensor_reduce(out=neg_max[:], in_=banks["s", n][:], axis=AXIS.X, op=ALU.max, negate=True)
            staged["neg_max", n] = neg_max

        def exponent(n):
            weights = soft.tile([P, COLS], F32, tag="weights")
            total = soft.tile([P, 1], F32, tag="total")
            nc.scalar.activation(out=weights[:], in_=banks["s", n][:], func=ACT.Exp, bias=staged["neg_max", n][:, 0:1], scale=1.0, accum_out=total[:])
            staged["weights", n] = weights
            staged["total", n] = total

        def invert(n):
            inverse = soft.tile([P, 1], F32, tag="inverse")
            nc.vector.reciprocal(out=inverse[:], in_=staged["total", n][:])
            staged["inverse", n] = inverse

        def normalise(n):
            block, h = n // HEADS, n % HEADS
            weights = staged["weights", n]
            nc.vector.tensor_scalar_mul(out=weights[:], in0=weights[:], scalar1=staged["inverse", n][:, 0:1])
            nc.sync.dma_start(out=out_rows[h, block * P : (block + 1) * P, :], in_=weights[:])

        def softmax_stages(n):
            if 0 <= n - 4 < PIECES:
                normalise(n - 4)
            if 0 <= n - 3 < PIECES:
                invert(n - 3)
            if 0 <= n - 2 < PIECES:
                exponent(n - 2)
            if 0 <= n - 1 < PIECES:
                row_max(n - 1)
            if 0 <= n < PIECES:
                scores(n)

        def idle_matmuls(count, moving):
            idle_bank = psum.tile([P, COLS], F32, tag="bank")
            for i in range(count):
                nc.tensor.matmul(out=idle_bank[:], lhsT=ident_bf16[:], rhs=moving, start=True, stop=True)

        idle_matmuls(WARM_FIRST, zero_rows[:])
        for v in range(PASSES + PREPARE_STAGES - 1):
            x_stages(v, 0, PASSES)
        for g in range(PASSES):
            for group in range(HEAD_GROUPS):
                w_regroup(g, group)
        idle_matmuls(WARM_SECOND, staged["w", 0, 0][:, 0:P, :].rearrange("p c t -> p (c t)"))
        for group in range(HEAD_GROUPS):
            for g in range(PASSES):
                w_quantise(g, group)
        bias_bank = psum.tile([P, P], BF16, tag="bank")
        nc.tensor.transpose(bias_bank[:], bias_rows[:], ident_bf16[:])
        bias_scaled = const.tile([P, HEADS], F32)
        nc.vector.tensor_scalar_mul(out=bias_scaled[:], in0=bias_bank[:, 0:HEADS], scalar1=factor)
        for n in range(LOOKAHEAD + PREPARE_STAGES - 1):
            q_stages(n, 0, LOOKAHEAD)
        for bank_no in range(K_BANKS + PREPARE_STAGES - 1):
            k_stages(bank_no, 0, K_BANKS)
        for n in range(PIECES + SOFTMAX_STAGES - 1):
            block, h = n // HEADS, n % HEADS
            if block + 1 < COL_BLOCKS and h < PASSES + PREPARE_STAGES - 1:
                x_stages(PASSES * (block + 1) + h, PASSES * (block + 1), PASSES * (block + 2))
            q_stages(n + LOOKAHEAD, LOOKAHEAD, PIECES)
            softmax_stages(n)
